import numpy as np
import ml_dtypes


def mxq(x, axis, fmt="e4m3"):
    dtype, down = {"e4m3": (ml_dtypes.float8_e4m3fn, 7), "e5m2": (ml_dtypes.float8_e5m2, 14)}[fmt]
    v = np.moveaxis(np.asarray(x, np.float32).astype(ml_dtypes.bfloat16).astype(np.float64), axis, -1)
    blocks = v.reshape(v.shape[:-1] + (-1, 32))
    amax = np.abs(blocks).max(-1, keepdims=True)
    byte = np.maximum(np.where(amax > 0, np.frexp(amax)[1] - 1 + 127, 0) - down, 1)
    scale = np.exp2(byte - 127.0)
    codes = (blocks / scale).astype(np.float32).astype(dtype).astype(np.float64)
    return np.moveaxis((codes * scale).reshape(v.shape), -1, axis)


WIDE = False


def mx_kscale(k):
    if not WIDE:
        return np.ones(k)
    levels = np.array([10, -10, 5, -5, 0])
    a = np.random.permutation(np.resize(levels, k // 512 * 4)).reshape(k // 512, 4)
    idx = np.arange(k)
    return np.exp2(a[idx // 512, idx % 128 // 32])


BF16 = ml_dtypes.bfloat16


def bf(x):
    return np.asarray(x, np.float32).astype(BF16)


def f64(x):
    return np.asarray(x).astype(np.float64)


B, L, D, E, W1, C, F_LEN = 2, 1024, 511, 512, 8, 256, 4
SR = 0.55
WS = 0.7
KEEP = 0.75


def setup_inputs():
    s = mx_kscale(E)
    st = np.random.standard_normal((B, L, E)) * SR
    st[..., 0] = 1.0
    return {"state": bf(st * s),
            "Wg": bf(np.random.standard_normal((C, W1, E)) * WS / np.sqrt(E) / s),
            "Mg": bf(np.random.random((C, W1, E)) < KEEP),
            "bg": bf(1.0 + 0.1 * np.random.standard_normal((C, W1)))}


def reference(state, Wg, Mg, bg):
    wm = f64(Wg) * f64(Mg)
    sq = mxq(f64(state).reshape(B * L, E), 1, "e4m3")
    wq = mxq(wm.reshape(C * W1, E), 1, "e4m3")
    h = (sq @ wq.T).reshape(B, L, C, W1) + f64(bg)
    return np.prod(h, axis=-1)

@@ -1,0 +1,222 @@
+from contextlib import ExitStack
+
+import concourse.mybir as mybir
+from concourse.masks import make_identity
+
+F32 = mybir.dt.float32
+BF16 = mybir.dt.bfloat16
+U32 = mybir.dt.uint32
+U8 = mybir.dt.uint8
+FP8X4 = mybir.dt.float8_e4m3fn_x4
+ADD = mybir.AluOpType.add
+MULT = mybir.AluOpType.mult
+IDENTITY = mybir.ActivationFunctionType.Identity
+
+P = 128
+E = 512
+TOKENS = 2048
+CHANNELS = 256
+FORMS = 8
+ROWS = 4
+UNIT = ROWS * P
+TOKEN_CHUNKS = TOKENS // UNIT
+CHANNEL_HALVES = CHANNELS // P
+GROUPS = CHANNEL_HALVES * TOKEN_CHUNKS
+SCALAR_FORMS = 3
+OUT_LAG = 2
+
+FLOPS = 2 * TOKENS * CHANNELS * FORMS * E
+
+
+def tile_ac_filter_prenorm_net_nd_pa_kernel(tc, state, Wg, Mg, bg, out):
+    nc = tc.nc
+    state_rows = state.flatten_outer_dims().rearrange("(q n) e -> q n e", q=P)
+    out_rows = out.flatten_outer_dims().rearrange("(q n) c -> q n c", q=P)
+    wg_rows = Wg.rearrange("(h c) j e -> h c j e", c=P)
+    mg_rows = Mg.rearrange("(h c) j e -> h c j e", c=P)
+
+    with ExitStack() as ctx:
+        ctx.enter_context(tc.manual_schedule())
+        keep = ctx.enter_context(tc.tile_pool(name="keep", bufs=1))
+        chains = ctx.enter_context(tc.tile_pool(name="chains", bufs=OUT_LAG + 2))
+        stage = ctx.enter_context(tc.tile_pool(name="stage", bufs=3))
+        form_banks = ctx.enter_context(tc.psum_pool(name="form_banks", bufs=6))
+        turn_banks = ctx.enter_context(tc.psum_pool(name="turn_banks", bufs=2))
+
+        bias_bf16 = keep.tile([P, CHANNEL_HALVES, FORMS], BF16)
+        nc.scalar.dma_start(out=bias_bf16[:], in_=bg.rearrange("(h c) j -> c h j", c=P))
+
+        def load_weights(half, quad):
+            forms = slice(quad * ROWS, (quad + 1) * ROWS)
+            w = keep.tile([P, ROWS, E], BF16, name="w%d%d" % (half, quad))
+            m = keep.tile([P, ROWS, E], BF16, name="m%d%d" % (half, quad))
+            nc.sync.dma_start(out=w[:], in_=wg_rows[half, :, forms, :])
+            nc.sync.dma_start(out=m[:], in_=mg_rows[half, :, forms, :])
+            return w, m
+
+        def load_state(chunk):
+            s = keep.tile([P, ROWS, E], BF16, name="s%d" % chunk)
+            nc.sync.dma_start(out=s[:], in_=state_rows[:, chunk * ROWS : (chunk + 1) * ROWS, :])
+            return s
+
+        weights = {}
+        states = {}
+        weights[(0, 0)] = load_weights(0, 0)
+        weights[(0, 1)] = load_weights(0, 1)
+        for chunk in range(TOKEN_CHUNKS):
+            states[chunk] = load_state(chunk)
+        weights[(1, 0)] = load_weights(1, 0)
+        weights[(1, 1)] = load_weights(1, 1)
+
+        identity = keep.tile([P, P], F32)
+        make_identity(nc, identity[:])
+        bias = keep.tile([P, CHANNEL_HALVES * FORMS], F32)
+        nc.vector.tensor_copy(out=bias[:], in_=bias_bf16[:].rearrange("c h j -> c (h j)"))
+
+        w_codes = keep.tile([P, CHANNEL_HALVES * FORMS * P], U32, align_bytes=64)
+        w_scales = keep.tile([P, CHANNEL_HALVES * FORMS * P], U8, align_bytes=64)
+        s_codes = keep.tile([P, TOKENS], U32, align_bytes=64)
+        s_scales = keep.tile([P, TOKENS], U8, align_bytes=64)
+
+        def mask(half, quad):
+            w, m = weights[(half, quad)]
+            nc.vector.tensor_tensor(out=w[:], in0=w[:], in1=m[:], op=MULT)
+
+        def turn(rows, name):
+            words = rows[:].bitcast(F32)
+            grouped = keep.tile([P, ROWS, P, 4], BF16, name=name, align_bytes=64)
+            grouped_words = grouped[:].bitcast(F32)
+            for pair in range(ROWS // 2):
+                turned = turn_banks.tile([P, 2, 2, P], F32, tag="turn")
+                for a in range(2):
+                    for u in range(2):
+                        nc.tensor.transpose(
+                            turned[:, a, u, :],
+                            words[:, 2 * pair + a, u * P : (u + 1) * P],
+                            identity[:],
+                        )
+                nc.scalar.copy(
+                    out=grouped_words[:, 2 * pair : 2 * pair + 2, :, :],
+                    in_=turned[:].rearrange("p a u r -> p a r u"),
+                )
+            return grouped
+
+        def quantise(grouped, codes, scales):
+            nc.vector.quantize_mx(
+                out=codes.bitcast(FP8X4),
+                scales=scales,
+                in_=grouped[:].rearrange("p a r t -> p (a r t)"),
+            )
+
+        grouped_units = {}
+
+        def turn_unit(unit):
+            kind, i, k = unit
+            rows = states[i] if kind == "state" else weights[(i, k)][0]
+            grouped_units[unit] = turn(rows, "g_%s%d%d" % unit)
+
+        def quantise_unit(unit):
+            kind, i, k = unit
+            first = i * UNIT if kind == "state" else (2 * i + k) * UNIT
+            columns = slice(first, first + UNIT)
+            if kind == "state":
+                quantise(grouped_units[unit], s_codes[:, columns], s_scales[:, columns])
+            else:
+                quantise(grouped_units[unit], w_codes[:, columns], w_scales[:, columns])
+
+        def form_pass(group, j):
+            half, chunk = divmod(group, TOKEN_CHUNKS)
+            w_columns = slice((half * FORMS + j) * P, (half * FORMS + j + 1) * P)
+            s_columns = slice(chunk * UNIT, (chunk + 1) * UNIT)
+            bank = form_banks.tile([P, UNIT], F32, tag="form")
+            nc.tensor.matmul_mx(
+                out=bank[:],
+                lhsT=w_codes[:, w_columns].bitcast(FP8X4),
+                lhsT_scale=w_scales[:, w_columns],
+                rhs=s_codes[:, s_columns].bitcast(FP8X4),
+                rhs_scale=s_scales[:, s_columns],
+                start=True,
+                stop=True,
+            )
+            return bank, bias[:, half * FORMS + j : half * FORMS + j + 1]
+
+        products = {}
+
+        def scalar_form(group, j):
+            bank, b = form_pass(group, j)
+            product = chains.tile([P, UNIT], F32, name="product%d" % j)
+            nc.scalar.activation(out=product[:], in_=bank[:], func=IDENTITY, bias=b, scale=1.0)
+            products[(group, j)] = product
+
+        def vector_form(group, j):
+            bank, b = form_pass(group, j)
+            product = products[(group, j % SCALAR_FORMS)]
+            nc.vector.scalar_tensor_tensor(
+                out=product[:], in0=bank[:], scalar=b, in1=product[:], op0=ADD, op1=MULT
+            )
+
+        def join(group, other):
+            nc.gpsimd.tensor_tensor(
+                out=products[(group, 0)][:],
+                in0=products[(group, 0)][:],
+                in1=products[(group, other)][:],
+                op=MULT,
+            )
+
+        def finish(group):
+            half, chunk = divmod(group, TOKEN_CHUNKS)
+            result = products[(group, 0)]
+            turned = turn_banks.tile([P, ROWS, P], F32, tag="turn")
+            for n in range(ROWS):
+                nc.tensor.transpose(turned[:, n, :], result[:, n * P : (n + 1) * P], identity[:])
+            rows = stage.tile([P, ROWS, P], F32)
+            nc.scalar.copy(out=rows[:], in_=turned[:])
+            nc.sync.dma_start(
+                out=out_rows[:, chunk * ROWS : (chunk + 1) * ROWS, half * P : (half + 1) * P],
+                in_=rows[:],
+            )
+
+        units = [("weights", 0, 0), ("weights", 0, 1), ("state", 0, 0), ("state", 1, 0), ("state", 2, 0)]
+        later_units = [("state", 3, 0), ("weights", 1, 0), ("weights", 1, 1)]
+
+        mask(0, 0)
+        turn_unit(units[0])
+        mask(0, 1)
+        turn_unit(units[1])
+        quantise_unit(units[0])
+        turn_unit(units[2])
+        quantise_unit(units[1])
+        turn_unit(units[3])
+        quantise_unit(units[2])
+        turn_unit(units[4])
+        quantise_unit(units[3])
+        for j in range(SCALAR_FORMS):
+            scalar_form(0, j)
+        quantise_unit(units[4])
+
+        for group in range(GROUPS):
+            unit = later_units[group] if group < len(later_units) else None
+            last_unit = later_units[group - 1] if 1 <= group <= len(later_units) else None
+            if unit is not None and unit[0] == "weights":
+                mask(unit[1], unit[2])
+            vector_form(group, 3)
+            vector_form(group, 4)
+            if last_unit is not None:
+                quantise_unit(last_unit)
+            vector_form(group, 5)
+            if group + 1 < GROUPS:
+                scalar_form(group + 1, 0)
+            vector_form(group, 6)
+            join(group, 2)
+            if group + 1 < GROUPS:
+                scalar_form(group + 1, 1)
+            vector_form(group, 7)
+            join(group, 1)
+            if group + 1 < GROUPS:
+                scalar_form(group + 1, 2)
+            if unit is not None:
+                turn_unit(unit)
+            if group >= OUT_LAG:
+                finish(group - OUT_LAG)
+        for group in range(GROUPS - OUT_LAG, GROUPS):
+            finish(group)

@@ -17,12 +17,18 @@ E = 512
 TOKENS = 2048
 CHANNELS = 256
 FORMS = 8
-ROWS = 4
-UNIT = ROWS * P
-TOKEN_CHUNKS = TOKENS // UNIT
+CHUNK = 512
+CHUNK_ROWS = CHUNK // P
+TOKEN_CHUNKS = TOKENS // CHUNK
 CHANNEL_HALVES = CHANNELS // P
 GROUPS = CHANNEL_HALVES * TOKEN_CHUNKS
-SCALAR_FORMS = 3
+UNIT_ROWS = 2
+UNIT = UNIT_ROWS * P
+FORM_PAIRS = FORMS // UNIT_ROWS
+SCALAR_FORMS = (0, 2, 4)
+VECTOR_FORMS = ((1, 0), (3, 1), (5, 2), (6, 0), (7, 1))
+
+QUANTISE_LAG = 3
 OUT_LAG = 2
 
 FLOPS = 2 * TOKENS * CHANNELS * FORMS * E
@@ -40,33 +46,39 @@ def tile_ac_filter_prenorm_net_nd_pa_kernel(tc, state, Wg, Mg, bg, out):
         keep = ctx.enter_context(tc.tile_pool(name="keep", bufs=1))
         chains = ctx.enter_context(tc.tile_pool(name="chains", bufs=OUT_LAG + 2))
         stage = ctx.enter_context(tc.tile_pool(name="stage", bufs=3))
-        form_banks = ctx.enter_context(tc.psum_pool(name="form_banks", bufs=6))
-        turn_banks = ctx.enter_context(tc.psum_pool(name="turn_banks", bufs=2))
+        banks = ctx.enter_context(tc.psum_pool(name="banks", bufs=8))
 
         bias_bf16 = keep.tile([P, CHANNEL_HALVES, FORMS], BF16)
         nc.scalar.dma_start(out=bias_bf16[:], in_=bg.rearrange("(h c) j -> c h j", c=P))
 
-        def load_weights(half, quad):
-            forms = slice(quad * ROWS, (quad + 1) * ROWS)
-            w = keep.tile([P, ROWS, E], BF16, name="w%d%d" % (half, quad))
-            m = keep.tile([P, ROWS, E], BF16, name="m%d%d" % (half, quad))
-            nc.sync.dma_start(out=w[:], in_=wg_rows[half, :, forms, :])
-            nc.sync.dma_start(out=m[:], in_=mg_rows[half, :, forms, :])
-            return w, m
+        state_tiles = {}
+        weight_tiles = {}
 
         def load_state(chunk):
-            s = keep.tile([P, ROWS, E], BF16, name="s%d" % chunk)
-            nc.sync.dma_start(out=s[:], in_=state_rows[:, chunk * ROWS : (chunk + 1) * ROWS, :])
-            return s
+            s = keep.tile([P, CHUNK_ROWS, E], BF16, name="s%d" % chunk)
+            nc.sync.dma_start(
+                out=s[:], in_=state_rows[:, chunk * CHUNK_ROWS : (chunk + 1) * CHUNK_ROWS, :]
+            )
+            state_tiles[chunk] = s
 
-        weights = {}
-        states = {}
-        weights[(0, 0)] = load_weights(0, 0)
-        weights[(0, 1)] = load_weights(0, 1)
-        for chunk in range(TOKEN_CHUNKS):
-            states[chunk] = load_state(chunk)
-        weights[(1, 0)] = load_weights(1, 0)
-        weights[(1, 1)] = load_weights(1, 1)
+        def load_weights(half, pair):
+            forms = slice(pair * UNIT_ROWS, (pair + 1) * UNIT_ROWS)
+            w = keep.tile([P, UNIT_ROWS, E], BF16, name="w%d%d" % (half, pair))
+            m = keep.tile([P, UNIT_ROWS, E], BF16, name="m%d%d" % (half, pair))
+            nc.sync.dma_start(out=w[:], in_=wg_rows[half, :, forms, :])
+            nc.sync.dma_start(out=m[:], in_=mg_rows[half, :, forms, :])
+            weight_tiles[(half, pair)] = (w, m)
+
+        load_state(0)
+        load_weights(0, 0)
+        load_weights(0, 1)
+        load_state(1)
+        load_weights(0, 2)
+        load_weights(0, 3)
+        load_state(2)
+        load_state(3)
+        for pair in range(FORM_PAIRS):
+            load_weights(1, pair)
 
         identity = keep.tile([P, P], F32)
         make_identity(nc, identity[:])
@@ -78,57 +90,45 @@ def tile_ac_filter_prenorm_net_nd_pa_kernel(tc, state, Wg, Mg, bg, out):
         s_codes = keep.tile([P, TOKENS], U32, align_bytes=64)
         s_scales = keep.tile([P, TOKENS], U8, align_bytes=64)
 
-        def mask(half, quad):
-            w, m = weights[(half, quad)]
-            nc.vector.tensor_tensor(out=w[:], in0=w[:], in1=m[:], op=MULT)
+        grouped_tiles = {}
 
-        def turn(rows, name):
-            words = rows[:].bitcast(F32)
-            grouped = keep.tile([P, ROWS, P, 4], BF16, name=name, align_bytes=64)
-            grouped_words = grouped[:].bitcast(F32)
-            for pair in range(ROWS // 2):
-                turned = turn_banks.tile([P, 2, 2, P], F32, tag="turn")
-                for a in range(2):
-                    for u in range(2):
-                        nc.tensor.transpose(
-                            turned[:, a, u, :],
-                            words[:, 2 * pair + a, u * P : (u + 1) * P],
-                            identity[:],
-                        )
-                nc.scalar.copy(
-                    out=grouped_words[:, 2 * pair : 2 * pair + 2, :, :],
-                    in_=turned[:].rearrange("p a u r -> p a r u"),
-                )
-            return grouped
+        def mask(unit):
+            kind, half, pair = unit
+            if kind == "weights":
+                w, m = weight_tiles[(half, pair)]
+                nc.vector.tensor_tensor(out=w[:], in0=w[:], in1=m[:], op=MULT)
 
-        def quantise(grouped, codes, scales):
-            nc.vector.quantize_mx(
-                out=codes.bitcast(FP8X4),
-                scales=scales,
-                in_=grouped[:].rearrange("p a r t -> p (a r t)"),
-            )
-
-        grouped_units = {}
-
-        def turn_unit(unit):
+        def turn(unit):
             kind, i, k = unit
-            rows = states[i] if kind == "state" else weights[(i, k)][0]
-            grouped_units[unit] = turn(rows, "g_%s%d%d" % unit)
-
-        def quantise_unit(unit):
-            kind, i, k = unit
-            first = i * UNIT if kind == "state" else (2 * i + k) * UNIT
-            columns = slice(first, first + UNIT)
             if kind == "state":
-                quantise(grouped_units[unit], s_codes[:, columns], s_scales[:, columns])
+                rows = state_tiles[i][:, k * UNIT_ROWS : (k + 1) * UNIT_ROWS, :]
             else:
-                quantise(grouped_units[unit], w_codes[:, columns], w_scales[:, columns])
+                rows = weight_tiles[(i, k)][0][:]
+            words = rows.bitcast(F32)
+            turned = banks.tile([P, UNIT_ROWS, 2, P], F32, tag="bank")
+            for a in range(UNIT_ROWS):
+                for u in range(2):
+                    nc.tensor.transpose(turned[:, a, u, :], words[:, a, u * P : (u + 1) * P], identity[:])
+            grouped = keep.tile([P, UNIT_ROWS, P, 4], BF16, name="grouped_%s%d%d" % unit, align_bytes=64)
+            nc.scalar.copy(out=grouped[:].bitcast(F32), in_=turned[:].rearrange("p a u r -> p a r u"))
+            grouped_tiles[unit] = grouped
+
+        def quantise(unit):
+            kind, i, k = unit
+            codes, scales = (s_codes, s_scales) if kind == "state" else (w_codes, w_scales)
+            units_before = i * (CHUNK // UNIT) + k if kind == "state" else i * FORM_PAIRS + k
+            columns = slice(units_before * UNIT, (units_before + 1) * UNIT)
+            nc.vector.quantize_mx(
+                out=codes[:, columns].bitcast(FP8X4),
+                scales=scales[:, columns],
+                in_=grouped_tiles[unit][:].rearrange("p a r t -> p (a r t)"),
+            )
 
         def form_pass(group, j):
             half, chunk = divmod(group, TOKEN_CHUNKS)
             w_columns = slice((half * FORMS + j) * P, (half * FORMS + j + 1) * P)
-            s_columns = slice(chunk * UNIT, (chunk + 1) * UNIT)
-            bank = form_banks.tile([P, UNIT], F32, tag="form")
+            s_columns = slice(chunk * CHUNK, (chunk + 1) * CHUNK)
+            bank = banks.tile([P, CHUNK], F32, tag="bank")
             nc.tensor.matmul_mx(
                 out=bank[:],
                 lhsT=w_codes[:, w_columns].bitcast(FP8X4),
@@ -142,80 +142,78 @@ def tile_ac_filter_prenorm_net_nd_pa_kernel(tc, state, Wg, Mg, bg, out):
 
         products = {}
 
-        def scalar_form(group, j):
-            bank, b = form_pass(group, j)
-            product = chains.tile([P, UNIT], F32, name="product%d" % j)
-            nc.scalar.activation(out=product[:], in_=bank[:], func=IDENTITY, bias=b, scale=1.0)
-            products[(group, j)] = product
+        def scalar_forms(group):
+            for k, j in enumerate(SCALAR_FORMS):
+                bank, b = form_pass(group, j)
+                product = chains.tile([P, CHUNK], F32, name="product%d" % k)
+                nc.scalar.activation(out=product[:], in_=bank[:], func=IDENTITY, bias=b, scale=1.0)
+                products[(group, k)] = product
 
-        def vector_form(group, j):
+        def vector_form(group, j, k):
             bank, b = form_pass(group, j)
-            product = products[(group, j % SCALAR_FORMS)]
+            product = products[(group, k)]
             nc.vector.scalar_tensor_tensor(
                 out=product[:], in0=bank[:], scalar=b, in1=product[:], op0=ADD, op1=MULT
             )
 
-        def join(group, other):
-            nc.gpsimd.tensor_tensor(
-                out=products[(group, 0)][:],
-                in0=products[(group, 0)][:],
-                in1=products[(group, other)][:],
-                op=MULT,
-            )
+        def join(group, k):
+            joiner = nc.vector if group == GROUPS - 1 else nc.gpsimd
+            result = products[(group, 0)]
+            joiner.tensor_tensor(out=result[:], in0=result[:], in1=products[(group, k)][:], op=MULT)
 
         def finish(group):
             half, chunk = divmod(group, TOKEN_CHUNKS)
             result = products[(group, 0)]
-            turned = turn_banks.tile([P, ROWS, P], F32, tag="turn")
-            for n in range(ROWS):
+            turned = banks.tile([P, CHUNK_ROWS, P], F32, tag="bank")
+            for n in range(CHUNK_ROWS):
                 nc.tensor.transpose(turned[:, n, :], result[:, n * P : (n + 1) * P], identity[:])
-            rows = stage.tile([P, ROWS, P], F32)
+            rows = stage.tile([P, CHUNK_ROWS, P], F32)
             nc.scalar.copy(out=rows[:], in_=turned[:])
             nc.sync.dma_start(
-                out=out_rows[:, chunk * ROWS : (chunk + 1) * ROWS, half * P : (half + 1) * P],
+                out=out_rows[:, chunk * CHUNK_ROWS : (chunk + 1) * CHUNK_ROWS, half * P : (half + 1) * P],
                 in_=rows[:],
             )
 
-        units = [("weights", 0, 0), ("weights", 0, 1), ("state", 0, 0), ("state", 1, 0), ("state", 2, 0)]
-        later_units = [("state", 3, 0), ("weights", 1, 0), ("weights", 1, 1)]
+        first_units = [
+            ("state", 0, 0),
+            ("state", 0, 1),
+            ("weights", 0, 0),
+            ("weights", 0, 1),
+            ("state", 1, 0),
+            ("state", 1, 1),
+            ("weights", 0, 2),
+            ("weights", 0, 3),
+        ]
+        later_units = {
+            0: [("state", 2, 0), ("state", 2, 1), ("state", 3, 0), ("state", 3, 1)],
+            1: [("weights", 1, 0), ("weights", 1, 1)],
+            2: [("weights", 1, 2), ("weights", 1, 3)],
+        }
 
-        mask(0, 0)
-        turn_unit(units[0])
-        mask(0, 1)
-        turn_unit(units[1])
-        quantise_unit(units[0])
-        turn_unit(units[2])
-        quantise_unit(units[1])
-        turn_unit(units[3])
-        quantise_unit(units[2])
-        turn_unit(units[4])
-        quantise_unit(units[3])
-        for j in range(SCALAR_FORMS):
-            scalar_form(0, j)
-        quantise_unit(units[4])
+        for i in range(len(first_units) + QUANTISE_LAG):
+            if i < len(first_units):
+                mask(first_units[i])
+                turn(first_units[i])
+            if i >= QUANTISE_LAG:
+                quantise(first_units[i - QUANTISE_LAG])
+        scalar_forms(0)
 
         for group in range(GROUPS):
-            unit = later_units[group] if group < len(later_units) else None
-            last_unit = later_units[group - 1] if 1 <= group <= len(later_units) else None
-            if unit is not None and unit[0] == "weights":
-                mask(unit[1], unit[2])
-            vector_form(group, 3)
-            vector_form(group, 4)
-            if last_unit is not None:
-                quantise_unit(last_unit)
-            vector_form(group, 5)
+            for unit in later_units.get(group, []):
+                mask(unit)
+            for step, (j, k) in enumerate(VECTOR_FORMS):
+                if step == 2:
+                    for unit in later_units.get(group - 1, []):
+                        quantise(unit)
+                vector_form(group, j, k)
+                if j == 6:
+                    join(group, 2)
+                if j == 7:
+                    join(group, 1)
             if group + 1 < GROUPS:
-                scalar_form(group + 1, 0)
-            vector_form(group, 6)
-            join(group, 2)
-            if group + 1 < GROUPS:
-                scalar_form(group + 1, 1)
-            vector_form(group, 7)
-            join(group, 1)
-            if group + 1 < GROUPS:
-                scalar_form(group + 1, 2)
-            if unit is not None:
-                turn_unit(unit)
+                scalar_forms(group + 1)
+            for unit in later_units.get(group, []):
+                turn(unit)
             if group >= OUT_LAG:
                 finish(group - OUT_LAG)
         for group in range(GROUPS - OUT_LAG, GROUPS):

@@ -157,9 +157,8 @@ def tile_ac_filter_prenorm_net_nd_pa_kernel(tc, state, Wg, Mg, bg, out):
             )
 
         def join(group, k):
-            joiner = nc.vector if group == GROUPS - 1 else nc.gpsimd
             result = products[(group, 0)]
-            joiner.tensor_tensor(out=result[:], in0=result[:], in1=products[(group, k)][:], op=MULT)
+            nc.vector.tensor_tensor(out=result[:], in0=result[:], in1=products[(group, k)][:], op=MULT)
 
         def finish(group):
             half, chunk = divmod(group, TOKEN_CHUNKS)

from contextlib import ExitStack

import concourse.mybir as mybir
from concourse.masks import make_identity

F32 = mybir.dt.float32
BF16 = mybir.dt.bfloat16
U32 = mybir.dt.uint32
U8 = mybir.dt.uint8
FP8X4 = mybir.dt.float8_e4m3fn_x4
ADD = mybir.AluOpType.add
MULT = mybir.AluOpType.mult
IDENTITY = mybir.ActivationFunctionType.Identity

P = 128
E = 512
TOKENS = 2048
CHANNELS = 256
FORMS = 8
CHUNK = 512
CHUNK_ROWS = CHUNK // P
TOKEN_CHUNKS = TOKENS // CHUNK
CHANNEL_HALVES = CHANNELS // P
GROUPS = CHANNEL_HALVES * TOKEN_CHUNKS
UNIT_ROWS = 2
UNIT = UNIT_ROWS * P
FORM_PAIRS = FORMS // UNIT_ROWS
SCALAR_FORMS = (0, 2, 4)
VECTOR_FORMS = ((1, 0), (3, 1), (5, 2), (6, 0), (7, 1))

QUANTISE_LAG = 3
OUT_LAG = 2

FLOPS = 2 * TOKENS * CHANNELS * FORMS * E


def tile_ac_filter_prenorm_net_nd_pa_kernel(tc, state, Wg, Mg, bg, out):
    nc = tc.nc
    state_rows = state.flatten_outer_dims().rearrange("(q n) e -> q n e", q=P)
    out_rows = out.flatten_outer_dims().rearrange("(q n) c -> q n c", q=P)
    wg_rows = Wg.rearrange("(h c) j e -> h c j e", c=P)
    mg_rows = Mg.rearrange("(h c) j e -> h c j e", c=P)

    with ExitStack() as ctx:
        ctx.enter_context(tc.manual_schedule())
        keep = ctx.enter_context(tc.tile_pool(name="keep", bufs=1))
        chains = ctx.enter_context(tc.tile_pool(name="chains", bufs=OUT_LAG + 2))
        stage = ctx.enter_context(tc.tile_pool(name="stage", bufs=3))
        banks = ctx.enter_context(tc.psum_pool(name="banks", bufs=8))

        bias_bf16 = keep.tile([P, CHANNEL_HALVES, FORMS], BF16)
        nc.scalar.dma_start(out=bias_bf16[:], in_=bg.rearrange("(h c) j -> c h j", c=P))

        state_tiles = {}
        weight_tiles = {}

        def load_state(chunk):
            s = keep.tile([P, CHUNK_ROWS, E], BF16, name="s%d" % chunk)
            nc.sync.dma_start(
                out=s[:], in_=state_rows[:, chunk * CHUNK_ROWS : (chunk + 1) * CHUNK_ROWS, :]
            )
            state_tiles[chunk] = s

        def load_weights(half, pair):
            forms = slice(pair * UNIT_ROWS, (pair + 1) * UNIT_ROWS)
            w = keep.tile([P, UNIT_ROWS, E], BF16, name="w%d%d" % (half, pair))
            m = keep.tile([P, UNIT_ROWS, E], BF16, name="m%d%d" % (half, pair))
            nc.sync.dma_start(out=w[:], in_=wg_rows[half, :, forms, :])
            nc.sync.dma_start(out=m[:], in_=mg_rows[half, :, forms, :])
            weight_tiles[(half, pair)] = (w, m)

        load_state(0)
        load_weights(0, 0)
        load_weights(0, 1)
        load_state(1)
        load_weights(0, 2)
        load_weights(0, 3)
        load_state(2)
        load_state(3)
        for pair in range(FORM_PAIRS):
            load_weights(1, pair)

        identity = keep.tile([P, P], F32)
        make_identity(nc, identity[:])
        bias = keep.tile([P, CHANNEL_HALVES * FORMS], F32)
        nc.vector.tensor_copy(out=bias[:], in_=bias_bf16[:].rearrange("c h j -> c (h j)"))

        w_codes = keep.tile([P, CHANNEL_HALVES * FORMS * P], U32, align_bytes=64)
        w_scales = keep.tile([P, CHANNEL_HALVES * FORMS * P], U8, align_bytes=64)
        s_codes = keep.tile([P, TOKENS], U32, align_bytes=64)
        s_scales = keep.tile([P, TOKENS], U8, align_bytes=64)

        grouped_tiles = {}

        def mask(unit):
            kind, half, pair = unit
            if kind == "weights":
                w, m = weight_tiles[(half, pair)]
                nc.vector.tensor_tensor(out=w[:], in0=w[:], in1=m[:], op=MULT)

        def turn(unit):
            kind, i, k = unit
            if kind == "state":
                rows = state_tiles[i][:, k * UNIT_ROWS : (k + 1) * UNIT_ROWS, :]
            else:
                rows = weight_tiles[(i, k)][0][:]
            words = rows.bitcast(F32)
            turned = banks.tile([P, UNIT_ROWS, 2, P], F32, tag="bank")
            for a in range(UNIT_ROWS):
                for u in range(2):
                    nc.tensor.transpose(turned[:, a, u, :], words[:, a, u * P : (u + 1) * P], identity[:])
            grouped = keep.tile([P, UNIT_ROWS, P, 4], BF16, name="grouped_%s%d%d" % unit, align_bytes=64)
            nc.scalar.copy(out=grouped[:].bitcast(F32), in_=turned[:].rearrange("p a u r -> p a r u"))
            grouped_tiles[unit] = grouped

        def quantise(unit):
            kind, i, k = unit
            codes, scales = (s_codes, s_scales) if kind == "state" else (w_codes, w_scales)
            units_before = i * (CHUNK // UNIT) + k if kind == "state" else i * FORM_PAIRS + k
            columns = slice(units_before * UNIT, (units_before + 1) * UNIT)
            nc.vector.quantize_mx(
                out=codes[:, columns].bitcast(FP8X4),
                scales=scales[:, columns],
                in_=grouped_tiles[unit][:].rearrange("p a r t -> p (a r t)"),
            )

        def form_pass(group, j):
            half, chunk = divmod(group, TOKEN_CHUNKS)
            w_columns = slice((half * FORMS + j) * P, (half * FORMS + j + 1) * P)
            s_columns = slice(chunk * CHUNK, (chunk + 1) * CHUNK)
            bank = banks.tile([P, CHUNK], F32, tag="bank")
            nc.tensor.matmul_mx(
                out=bank[:],
                lhsT=w_codes[:, w_columns].bitcast(FP8X4),
                lhsT_scale=w_scales[:, w_columns],
                rhs=s_codes[:, s_columns].bitcast(FP8X4),
                rhs_scale=s_scales[:, s_columns],
                start=True,
                stop=True,
            )
            return bank, bias[:, half * FORMS + j : half * FORMS + j + 1]

        products = {}

        def scalar_forms(group):
            for k, j in enumerate(SCALAR_FORMS):
                bank, b = form_pass(group, j)
                product = chains.tile([P, CHUNK], F32, name="product%d" % k)
                nc.scalar.activation(out=product[:], in_=bank[:], func=IDENTITY, bias=b, scale=1.0)
                products[(group, k)] = product

        def vector_form(group, j, k):
            bank, b = form_pass(group, j)
            product = products[(group, k)]
            nc.vector.scalar_tensor_tensor(
                out=product[:], in0=bank[:], scalar=b, in1=product[:], op0=ADD, op1=MULT
            )

        def join(group, k):
            result = products[(group, 0)]
            nc.vector.tensor_tensor(out=result[:], in0=result[:], in1=products[(group, k)][:], op=MULT)

        def finish(group):
            half, chunk = divmod(group, TOKEN_CHUNKS)
            result = products[(group, 0)]
            turned = banks.tile([P, CHUNK_ROWS, P], F32, tag="bank")
            for n in range(CHUNK_ROWS):
                nc.tensor.transpose(turned[:, n, :], result[:, n * P : (n + 1) * P], identity[:])
            rows = stage.tile([P, CHUNK_ROWS, P], F32)
            nc.scalar.copy(out=rows[:], in_=turned[:])
            nc.sync.dma_start(
                out=out_rows[:, chunk * CHUNK_ROWS : (chunk + 1) * CHUNK_ROWS, half * P : (half + 1) * P],
                in_=rows[:],
            )

        first_units = [
            ("state", 0, 0),
            ("state", 0, 1),
            ("weights", 0, 0),
            ("weights", 0, 1),
            ("state", 1, 0),
            ("state", 1, 1),
            ("weights", 0, 2),
            ("weights", 0, 3),
        ]
        later_units = {
            0: [("state", 2, 0), ("state", 2, 1), ("state", 3, 0), ("state", 3, 1)],
            1: [("weights", 1, 0), ("weights", 1, 1)],
            2: [("weights", 1, 2), ("weights", 1, 3)],
        }

        for i in range(len(first_units) + QUANTISE_LAG):
            if i < len(first_units):
                mask(first_units[i])
                turn(first_units[i])
            if i >= QUANTISE_LAG:
                quantise(first_units[i - QUANTISE_LAG])
        scalar_forms(0)

        for group in range(GROUPS):
            for unit in later_units.get(group, []):
                mask(unit)
            for step, (j, k) in enumerate(VECTOR_FORMS):
                if step == 2:
                    for unit in later_units.get(group - 1, []):
                        quantise(unit)
                vector_form(group, j, k)
                if j == 6:
                    join(group, 2)
                if j == 7:
                    join(group, 1)
            if group + 1 < GROUPS:
                scalar_forms(group + 1)
            for unit in later_units.get(group, []):
                turn(unit)
            if group >= OUT_LAG:
                finish(group - OUT_LAG)
        for group in range(GROUPS - OUT_LAG, GROUPS):
            finish(group)
